import numpy as np
import ml_dtypes


def mxq(x, axis, fmt="e4m3"):
    dtype, down = {"e4m3": (ml_dtypes.float8_e4m3fn, 7), "e5m2": (ml_dtypes.float8_e5m2, 14)}[fmt]
    v = np.moveaxis(np.asarray(x, np.float32).astype(ml_dtypes.bfloat16).astype(np.float64), axis, -1)
    blocks = v.reshape(v.shape[:-1] + (-1, 32))
    amax = np.abs(blocks).max(-1, keepdims=True)
    byte = np.maximum(np.where(amax > 0, np.frexp(amax)[1] - 1 + 127, 0) - down, 1)
    scale = np.exp2(byte - 127.0)
    codes = (blocks / scale).astype(np.float32).astype(dtype).astype(np.float64)
    return np.moveaxis((codes * scale).reshape(v.shape), -1, axis)


WIDE = False


def mx_kscale(k):
    if not WIDE:
        return np.ones(k)
    levels = np.array([10, -10, 5, -5, 0])
    a = np.random.permutation(np.resize(levels, k // 512 * 4)).reshape(k // 512, 4)
    idx = np.arange(k)
    return np.exp2(a[idx // 512, idx % 128 // 32])


BF16 = ml_dtypes.bfloat16


def bf(x):
    return np.asarray(x, np.float32).astype(BF16)


def f64(x):
    return np.asarray(x).astype(np.float64)


E2M1 = np.array([0.0, 0.5, 1.0, 1.5, 2.0, 3.0, 4.0, 6.0, -0.0, -0.5, -1.0, -1.5, -2.0, -3.0, -4.0, -6.0])


def pack_weight(w, fmt):
    k, n = w.shape
    w = f64(bf(w)).reshape(k // 32, 32, n)
    amax = np.abs(w).max(1)
    if fmt == "e4m3":
        byte = np.frexp(amax)[1] - 1 + 127 - 7
    else:
        mant, ex = np.frexp(amax / 6.0)
        byte = np.where(mant > 0.5, ex, ex - 1) + 127
    byte = np.clip(np.where(amax > 0, byte, 1), 1, 254)
    scaled = (w * np.exp2(127.0 - byte)[:, None, :]).reshape(k, n).astype(np.float32)
    by_word = np.ascontiguousarray(scaled.reshape(k // 512, 128, 4, n).transpose(0, 1, 3, 2))
    if fmt == "e4m3":
        words = by_word.astype(ml_dtypes.float8_e4m3fn).view(np.uint8)
    else:
        c = by_word.astype(ml_dtypes.float4_e2m1fn).view(np.uint8) & 0xF
        words = c[..., 0::2] | (c[..., 1::2] << 4)
    return np.ascontiguousarray(words), np.ascontiguousarray(byte.astype(np.uint8).reshape(k // 512, 16, n))


def unpack_weight(words, scales, fmt):
    g, p, n, _ = words.shape
    if fmt == "e4m3":
        vals = np.ascontiguousarray(words).view(ml_dtypes.float8_e4m3fn).astype(np.float64)
    else:
        nib = np.empty((g, p, n, 4), np.uint8)
        nib[..., 0::2] = words & 0xF
        nib[..., 1::2] = words >> 4
        vals = E2M1[nib]
    vals = vals * np.repeat(np.exp2(scales.astype(np.float64) - 127.0), 8, axis=1)[..., None]
    return vals.transpose(0, 1, 3, 2).reshape(g * 512, n)


M, I0, I1, I2, N0, N1, N2 = 512, 1024, 2048, 4096, 1024, 1024, 2048
FMT = "e4m3"


def block(fan_in, fan_out, s):
    return pack_weight(np.random.uniform(-1.0, 1.0, (fan_in, fan_out)) / np.sqrt(fan_in) / s[:fan_in, None], FMT)


def setup_inputs():
    s = mx_kscale(I2)
    x = bf(np.random.standard_normal((M, I2)) * s)
    w0_words, w0_scales = block(I0, N0, s)
    w1_words, w1_scales = block(I1, N1, s)
    w2_words, w2_scales = block(I2, N2, s)
    bias = bf(np.random.standard_normal(N0 + N1 + N2) * 0.1)
    return {"x": x,
            "w0_words": w0_words, "w0_scales": w0_scales,
            "w1_words": w1_words, "w1_scales": w1_scales,
            "w2_words": w2_words, "w2_scales": w2_scales,
            "bias": bias}


def reference(x, w0_words, w0_scales, w1_words, w1_scales, w2_words, w2_scales, bias):
    xq = mxq(f64(x), 1, "e4m3")
    y0 = xq[:, :I0] @ unpack_weight(w0_words, w0_scales, FMT)
    y1 = xq[:, :I1] @ unpack_weight(w1_words, w1_scales, FMT)
    y2 = xq[:, :I2] @ unpack_weight(w2_words, w2_scales, FMT)
    return np.concatenate([y0, y1, y2], axis=1) + f64(bias)

@@ -1,0 +1,168 @@
+from contextlib import ExitStack
+
+import concourse.mybir as mybir
+from concourse.masks import make_identity
+
+F32 = mybir.dt.float32
+BF16 = mybir.dt.bfloat16
+I32 = mybir.dt.int32
+U32 = mybir.dt.uint32
+U8 = mybir.dt.uint8
+FP8X4 = mybir.dt.float8_e4m3fn_x4
+
+P = 128
+K_PASS = 512
+N_TILE = 512
+TOKENS = 512
+TOKEN_TILES = TOKENS // P
+K_CHUNK = 1024
+CHUNK_PASSES = K_CHUNK // K_PASS
+X_CHUNKS = 4096 // K_CHUNK
+PASSES_PER_LOAD = 4
+PLANES_PER_TILE = 4
+LEAD = 5
+RESULT_BUFS = 16
+
+FLOPS = 2 * TOKENS * (1024 * 1024 + 2048 * 1024 + 4096 * 2048)
+
+
+def tile_mlinear_kernel(
+    tc, x, w0_words, w0_scales, w1_words, w1_scales, w2_words, w2_scales, bias, out
+):
+    nc = tc.nc
+    weights = [(w0_words, w0_scales), (w1_words, w1_scales), (w2_words, w2_scales)]
+    col_tiles = [(wi, nt) for wi in range(len(weights)) for nt in range(weights[wi][0].shape[2] // N_TILE)]
+
+    with ExitStack() as ctx:
+        keep = ctx.enter_context(tc.tile_pool(name="keep", bufs=1))
+        stage = ctx.enter_context(tc.tile_pool(name="stage", bufs=4))
+        results = ctx.enter_context(tc.tile_pool(name="results", bufs=RESULT_BUFS))
+        psum_xt = ctx.enter_context(tc.psum_pool(name="psum_xt", bufs=3))
+        psum_bias = ctx.enter_context(tc.psum_pool(name="psum_bias", bufs=1))
+        psum_acc = ctx.enter_context(tc.psum_pool(name="psum_acc", bufs=4))
+        ctx.enter_context(tc.manual_schedule())
+
+        x_rows = {}
+        x_codes = {}
+        x_scales = {}
+        w_codes = {}
+        w_planes = []
+
+        for wi in range(len(weights)):
+            passes, columns = weights[wi][0].shape[0], weights[wi][0].shape[2]
+            planes = keep.tile(
+                [P, (passes + PLANES_PER_TILE - 1) // PLANES_PER_TILE, columns],
+                U8,
+                name="w%d_planes" % wi,
+                align_bytes=64,
+            )
+            w_planes.append(planes)
+        nc.vector.memset(w_planes[0][:].bitcast(I32), 0)
+        bias_row = keep.tile([P, out.shape[1]], BF16, name="bias_row")
+        nc.vector.memset(bias_row[:].bitcast(I32), 0)
+        nc.scalar.dma_start(out=bias_row[0:1, :], in_=bias.rearrange("(o n) -> o n", o=1))
+        ones = keep.tile([P, P], BF16, name="ones")
+        nc.vector.memset(ones[:], 1.0)
+        nc.vector.memset(w_planes[1][:].bitcast(I32), 0)
+        nc.vector.memset(w_planes[2][:].bitcast(I32), 0)
+        ident = keep.tile([P, P], F32, name="ident")
+        make_identity(nc, ident[:])
+
+        def load_for_col_tile(j):
+            if j < X_CHUNKS:
+                for m in range(TOKEN_TILES):
+                    rows = keep.tile([P, K_CHUNK], BF16, name="x_rows_%d_%d" % (j, m))
+                    nc.sync.dma_start(
+                        out=rows[:], in_=x[m * P : (m + 1) * P, j * K_CHUNK : (j + 1) * K_CHUNK]
+                    )
+                    x_rows[(j, m)] = rows
+            wi, nt = col_tiles[j]
+            words, scales = weights[wi]
+            passes = words.shape[0]
+            if nt == 0:
+                scale_words = scales.bitcast(I32)
+                for h in range(0, passes, PLANES_PER_TILE):
+                    count = min(PLANES_PER_TILE, passes - h)
+                    for quadrant in range(4):
+                        first = 32 * quadrant
+                        nc.sync.dma_start(
+                            out=w_planes[wi][first : first + 4 * count, h // PLANES_PER_TILE, :].bitcast(I32),
+                            in_=scale_words[h : h + count, 4 * quadrant : 4 * quadrant + 4, :],
+                        )
+            by_partition = words.rearrange("g p n t -> p g (n t)").bitcast(I32)
+            for g0 in range(0, passes, PASSES_PER_LOAD):
+                count = min(PASSES_PER_LOAD, passes - g0)
+                codes = keep.tile([P, count, N_TILE], U32, name="w_codes_%d_%d" % (j, g0), align_bytes=64)
+                nc.sync.dma_start(
+                    out=codes[:].bitcast(I32),
+                    in_=by_partition[:, g0 : g0 + count, nt * N_TILE : (nt + 1) * N_TILE],
+                )
+                w_codes[(j, g0)] = codes
+
+        def quantise_x_chunk(c):
+            for m in range(TOKEN_TILES):
+                pairs = x_rows[(c, m)][:].bitcast(F32)
+                xt = psum_xt.tile([P, CHUNK_PASSES, 2, P], F32, name="xt")
+                for g in range(CHUNK_PASSES):
+                    for u in range(2):
+                        nc.tensor.transpose(
+                            xt[:, g, u, :], pairs[:, 256 * g + u : 256 * (g + 1) : 2], ident[:]
+                        )
+                grouped = stage.tile([P, CHUNK_PASSES * P * 4], BF16, name="grouped", align_bytes=64)
+                nc.scalar.copy(
+                    out=grouped[:].bitcast(F32).rearrange("p (g r u) -> p g r u", g=CHUNK_PASSES, u=2),
+                    in_=xt[:].rearrange("p g u r -> p g r u"),
+                )
+                codes = keep.tile([P, CHUNK_PASSES, P], U32, name="x_codes_%d_%d" % (c, m), align_bytes=64)
+                plane = keep.tile([P, CHUNK_PASSES, P], U8, name="x_scales_%d_%d" % (c, m), align_bytes=64)
+                nc.vector.quantize_mx(
+                    out=codes[:].rearrange("p g r -> p (g r)").bitcast(FP8X4),
+                    scales=plane[:].rearrange("p g r -> p (g r)"),
+                    in_=grouped[:],
+                )
+                x_codes[(c, m)] = codes
+                x_scales[(c, m)] = plane
+
+        def spread_bias(j):
+            bias_ps = psum_bias.tile([P, N_TILE], F32, name="bias_ps")
+            nc.tensor.matmul(
+                bias_ps[:], lhsT=ones[:], rhs=bias_row[:, j * N_TILE : (j + 1) * N_TILE], start=True, stop=True
+            )
+            bias_all = keep.tile([P, N_TILE], F32, name="bias_all_%d" % j)
+            nc.scalar.copy(out=bias_all[:], in_=bias_ps[:])
+            return bias_all
+
+        def multiply_col_tile(j, bias_all):
+            wi, nt = col_tiles[j]
+            passes = weights[wi][0].shape[0]
+            for m in range(TOKEN_TILES):
+                acc = psum_acc.tile([P, N_TILE], F32, name="acc")
+                for g in range(passes):
+                    c, g_in_chunk = divmod(g, CHUNK_PASSES)
+                    g0 = g - g % PASSES_PER_LOAD
+                    offset = 4 * (g % PLANES_PER_TILE)
+                    nc.tensor.matmul_mx(
+                        out=acc[:],
+                        lhsT=x_codes[(c, m)][:, g_in_chunk, :].bitcast(FP8X4),
+                        lhsT_scale=x_scales[(c, m)][:, g_in_chunk, :],
+                        rhs=w_codes[(j, g0)][:, g - g0, :].bitcast(FP8X4),
+                        rhs_scale=w_planes[wi][
+                            offset:P, g // PLANES_PER_TILE, nt * N_TILE : (nt + 1) * N_TILE
+                        ],
+                        start=(g == 0),
+                        stop=(g == passes - 1),
+                    )
+                result = results.tile([P, N_TILE], F32, name="result")
+                nc.vector.tensor_tensor(out=result[:], in0=acc[:], in1=bias_all[:], op=mybir.AluOpType.add)
+                nc.sync.dma_start(
+                    out=out[m * P : (m + 1) * P, j * N_TILE : (j + 1) * N_TILE], in_=result[:]
+                )
+
+        for j in range(LEAD):
+            load_for_col_tile(j)
+        for j in range(len(col_tiles)):
+            if j < X_CHUNKS:
+                quantise_x_chunk(j)
+            multiply_col_tile(j, spread_bias(j))
+            if j + LEAD < len(col_tiles):
+                load_for_col_tile(j + LEAD)

@@ -36,6 +36,7 @@ def tile_mlinear_kernel(
     with ExitStack() as ctx:
         keep = ctx.enter_context(tc.tile_pool(name="keep", bufs=1))
         stage = ctx.enter_context(tc.tile_pool(name="stage", bufs=4))
+        sorting = ctx.enter_context(tc.tile_pool(name="sorting", bufs=2 * TOKEN_TILES))
         results = ctx.enter_context(tc.tile_pool(name="results", bufs=RESULT_BUFS))
         psum_xt = ctx.enter_context(tc.psum_pool(name="psum_xt", bufs=3))
         psum_bias = ctx.enter_context(tc.psum_pool(name="psum_bias", bufs=1))
@@ -43,6 +44,7 @@ def tile_mlinear_kernel(
         ctx.enter_context(tc.manual_schedule())
 
         x_rows = {}
+        x_sorted = {}
         x_codes = {}
         x_scales = {}
         w_codes = {}
@@ -99,15 +101,21 @@ def tile_mlinear_kernel(
                 )
                 w_codes[(j, g0)] = codes
 
-        def quantise_x_chunk(c):
+        def sort_x_chunk(c):
             for m in range(TOKEN_TILES):
                 pairs = x_rows[(c, m)][:].bitcast(F32)
+                sorted_words = sorting.tile([P, CHUNK_PASSES, 2, P], F32, name="sorted_words")
+                nc.scalar.copy(
+                    out=sorted_words[:], in_=pairs.rearrange("r (g p u) -> r g u p", g=CHUNK_PASSES, u=2)
+                )
+                x_sorted[(c, m)] = sorted_words
+
+        def quantise_x_chunk(c):
+            for m in range(TOKEN_TILES):
                 xt = psum_xt.tile([P, CHUNK_PASSES, 2, P], F32, name="xt")
                 for g in range(CHUNK_PASSES):
                     for u in range(2):
-                        nc.tensor.transpose(
-                            xt[:, g, u, :], pairs[:, 256 * g + u : 256 * (g + 1) : 2], ident[:]
-                        )
+                        nc.tensor.transpose(xt[:, g, u, :], x_sorted[(c, m)][:, g, u, :], ident[:])
                 grouped = stage.tile([P, CHUNK_PASSES * P * 4], BF16, name="grouped", align_bytes=64)
                 nc.scalar.copy(
                     out=grouped[:].bitcast(F32).rearrange("p (g r u) -> p g r u", g=CHUNK_PASSES, u=2),
@@ -160,9 +168,13 @@ def tile_mlinear_kernel(
 
         for j in range(LEAD):
             load_for_col_tile(j)
+        sort_x_chunk(0)
         for j in range(len(col_tiles)):
             if j < X_CHUNKS:
                 quantise_x_chunk(j)
-            multiply_col_tile(j, spread_bias(j))
+            bias_all = spread_bias(j)
+            if j + 1 < X_CHUNKS:
+                sort_x_chunk(j + 1)
+            multiply_col_tile(j, bias_all)
             if j + LEAD < len(col_tiles):
                 load_for_col_tile(j + LEAD)

@@ -12,16 +12,16 @@ FP8X4 = mybir.dt.float8_e4m3fn_x4
 
 P = 128
 K_PASS = 512
-N_TILE = 512
+BANK = 512
+BLOCK = 1024
+BANKS = BLOCK // BANK
 TOKENS = 512
 TOKEN_TILES = TOKENS // P
 K_CHUNK = 1024
 CHUNK_PASSES = K_CHUNK // K_PASS
-X_CHUNKS = 4096 // K_CHUNK
-PASSES_PER_LOAD = 4
 PLANES_PER_TILE = 4
-LEAD = 5
-RESULT_BUFS = 16
+LEAD = 3
+RESULT_BUFS = 10
 
 FLOPS = 2 * TOKENS * (1024 * 1024 + 2048 * 1024 + 4096 * 2048)
 
@@ -31,15 +31,19 @@ def tile_mlinear_kernel(
 ):
     nc = tc.nc
     weights = [(w0_words, w0_scales), (w1_words, w1_scales), (w2_words, w2_scales)]
-    col_tiles = [(wi, nt) for wi in range(len(weights)) for nt in range(weights[wi][0].shape[2] // N_TILE)]
+    blocks = [(wi, nb) for wi in range(len(weights)) for nb in range(weights[wi][0].shape[2] // BLOCK)]
+    block_passes = [weights[wi][0].shape[0] for wi, nb in blocks]
+    new_chunks = [
+        range(0 if b == 0 else block_passes[b - 1] // CHUNK_PASSES, block_passes[b] // CHUNK_PASSES)
+        for b in range(len(blocks))
+    ]
 
     with ExitStack() as ctx:
         keep = ctx.enter_context(tc.tile_pool(name="keep", bufs=1))
         stage = ctx.enter_context(tc.tile_pool(name="stage", bufs=4))
-        sorting = ctx.enter_context(tc.tile_pool(name="sorting", bufs=2 * TOKEN_TILES))
+        x_pool = ctx.enter_context(tc.tile_pool(name="x_pool", bufs=2 * TOKEN_TILES))
         results = ctx.enter_context(tc.tile_pool(name="results", bufs=RESULT_BUFS))
-        psum_xt = ctx.enter_context(tc.psum_pool(name="psum_xt", bufs=3))
-        psum_bias = ctx.enter_context(tc.psum_pool(name="psum_bias", bufs=1))
+        psum_xt = ctx.enter_context(tc.psum_pool(name="psum_xt", bufs=4))
         psum_acc = ctx.enter_context(tc.psum_pool(name="psum_acc", bufs=4))
         ctx.enter_context(tc.manual_schedule())
 
@@ -70,18 +74,18 @@ def tile_mlinear_kernel(
         ident = keep.tile([P, P], F32, name="ident")
         make_identity(nc, ident[:])
 
-        def load_for_col_tile(j):
-            if j < X_CHUNKS:
+        def load_for_block(b):
+            for c in new_chunks[b]:
                 for m in range(TOKEN_TILES):
-                    rows = keep.tile([P, K_CHUNK], BF16, name="x_rows_%d_%d" % (j, m))
+                    rows = x_pool.tile([P, K_CHUNK], BF16, name="rows")
                     nc.sync.dma_start(
-                        out=rows[:], in_=x[m * P : (m + 1) * P, j * K_CHUNK : (j + 1) * K_CHUNK]
+                        out=rows[:], in_=x[m * P : (m + 1) * P, c * K_CHUNK : (c + 1) * K_CHUNK]
                     )
-                    x_rows[(j, m)] = rows
-            wi, nt = col_tiles[j]
+                    x_rows[(c, m)] = rows
+            wi, nb = blocks[b]
             words, scales = weights[wi]
-            passes = words.shape[0]
-            if nt == 0:
+            passes = block_passes[b]
+            if nb == 0:
                 scale_words = scales.bitcast(I32)
                 for h in range(0, passes, PLANES_PER_TILE):
                     count = min(PLANES_PER_TILE, passes - h)
@@ -91,90 +95,99 @@ def tile_mlinear_kernel(
                             out=w_planes[wi][first : first + 4 * count, h // PLANES_PER_TILE, :].bitcast(I32),
                             in_=scale_words[h : h + count, 4 * quadrant : 4 * quadrant + 4, :],
                         )
-            by_partition = words.rearrange("g p n t -> p g (n t)").bitcast(I32)
-            for g0 in range(0, passes, PASSES_PER_LOAD):
-                count = min(PASSES_PER_LOAD, passes - g0)
-                codes = keep.tile([P, count, N_TILE], U32, name="w_codes_%d_%d" % (j, g0), align_bytes=64)
+            for g in range(passes):
+                codes = keep.tile([P, BLOCK], U32, name="w_codes_%d_%d" % (b, g), align_bytes=64)
                 nc.sync.dma_start(
                     out=codes[:].bitcast(I32),
-                    in_=by_partition[:, g0 : g0 + count, nt * N_TILE : (nt + 1) * N_TILE],
+                    in_=words[g].rearrange("p n t -> p (n t)").bitcast(I32)[:, nb * BLOCK : (nb + 1) * BLOCK],
                 )
-                w_codes[(j, g0)] = codes
+                w_codes[(b, g)] = codes
 
-        def sort_x_chunk(c):
-            for m in range(TOKEN_TILES):
-                pairs = x_rows[(c, m)][:].bitcast(F32)
-                sorted_words = sorting.tile([P, CHUNK_PASSES, 2, P], F32, name="sorted_words")
-                nc.scalar.copy(
-                    out=sorted_words[:], in_=pairs.rearrange("r (g p u) -> r g u p", g=CHUNK_PASSES, u=2)
-                )
-                x_sorted[(c, m)] = sorted_words
+        def sort_x_for_block(b):
+            for c in new_chunks[b]:
+                for m in range(TOKEN_TILES):
+                    pairs = x_rows[(c, m)][:].bitcast(F32)
+                    sorted_words = x_pool.tile([P, CHUNK_PASSES, 2, P], F32, name="sorted_words")
+                    nc.scalar.copy(
+                        out=sorted_words[:], in_=pairs.rearrange("r (g p u) -> r g u p", g=CHUNK_PASSES, u=2)
+                    )
+                    x_sorted[(c, m)] = sorted_words
 
-        def quantise_x_chunk(c):
-            for m in range(TOKEN_TILES):
-                xt = psum_xt.tile([P, CHUNK_PASSES, 2, P], F32, name="xt")
-                for g in range(CHUNK_PASSES):
-                    for u in range(2):
-                        nc.tensor.transpose(xt[:, g, u, :], x_sorted[(c, m)][:, g, u, :], ident[:])
-                grouped = stage.tile([P, CHUNK_PASSES * P * 4], BF16, name="grouped", align_bytes=64)
-                nc.scalar.copy(
-                    out=grouped[:].bitcast(F32).rearrange("p (g r u) -> p g r u", g=CHUNK_PASSES, u=2),
-                    in_=xt[:].rearrange("p g u r -> p g r u"),
-                )
-                codes = keep.tile([P, CHUNK_PASSES, P], U32, name="x_codes_%d_%d" % (c, m), align_bytes=64)
-                plane = keep.tile([P, CHUNK_PASSES, P], U8, name="x_scales_%d_%d" % (c, m), align_bytes=64)
-                nc.vector.quantize_mx(
-                    out=codes[:].rearrange("p g r -> p (g r)").bitcast(FP8X4),
-                    scales=plane[:].rearrange("p g r -> p (g r)"),
-                    in_=grouped[:],
-                )
-                x_codes[(c, m)] = codes
-                x_scales[(c, m)] = plane
+        def quantise_x_for_block(b):
+            for c in new_chunks[b]:
+                for m in range(TOKEN_TILES):
+                    xt = psum_xt.tile([P, CHUNK_PASSES, 2, P], F32, name="xt")
+                    for g in range(CHUNK_PASSES):
+                        for u in range(2):
+                            nc.tensor.transpose(xt[:, g, u, :], x_sorted[(c, m)][:, g, u, :], ident[:])
+                    grouped = stage.tile([P, CHUNK_PASSES * P * 4], BF16, name="grouped", align_bytes=64)
+                    grouped_words = grouped[:].bitcast(F32).rearrange(
+                        "p (g r u) -> p g r u", g=CHUNK_PASSES, u=2
+                    )
+                    if m % 2 == 0:
+                        nc.scalar.copy(out=grouped_words, in_=xt[:].rearrange("p g u r -> p g r u"))
+                    else:
+                        nc.vector.tensor_copy(out=grouped_words, in_=xt[:].rearrange("p g u r -> p g r u"))
+                    codes = keep.tile(
+                        [P, CHUNK_PASSES, P], U32, name="x_codes_%d_%d" % (c, m), align_bytes=64
+                    )
+                    plane = keep.tile(
+                        [P, CHUNK_PASSES, P], U8, name="x_scales_%d_%d" % (c, m), align_bytes=64
+                    )
+                    nc.vector.quantize_mx(
+                        out=codes[:].rearrange("p g r -> p (g r)").bitcast(FP8X4),
+                        scales=plane[:].rearrange("p g r -> p (g r)"),
+                        in_=grouped[:],
+                    )
+                    x_codes[(c, m)] = codes
+                    x_scales[(c, m)] = plane
 
-        def spread_bias(j):
-            bias_ps = psum_bias.tile([P, N_TILE], F32, name="bias_ps")
-            nc.tensor.matmul(
-                bias_ps[:], lhsT=ones[:], rhs=bias_row[:, j * N_TILE : (j + 1) * N_TILE], start=True, stop=True
-            )
-            bias_all = keep.tile([P, N_TILE], F32, name="bias_all_%d" % j)
-            nc.scalar.copy(out=bias_all[:], in_=bias_ps[:])
+        def spread_bias(b):
+            bias_all = keep.tile([P, BLOCK], F32, name="bias_all_%d" % b)
+            for i in range(BANKS):
+                first = b * BLOCK + i * BANK
+                bias_ps = psum_acc.tile([P, BANK], F32, name="acc")
+                nc.tensor.matmul(
+                    bias_ps[:], lhsT=ones[:], rhs=bias_row[:, first : first + BANK], start=True, stop=True
+                )
+                nc.scalar.copy(out=bias_all[:, i * BANK : (i + 1) * BANK], in_=bias_ps[:])
             return bias_all
 
-        def multiply_col_tile(j, bias_all):
-            wi, nt = col_tiles[j]
-            passes = weights[wi][0].shape[0]
+        def multiply_block(b, bias_all):
+            wi, nb = blocks[b]
+            passes = block_passes[b]
             for m in range(TOKEN_TILES):
-                acc = psum_acc.tile([P, N_TILE], F32, name="acc")
+                accs = [psum_acc.tile([P, BANK], F32, name="acc") for i in range(BANKS)]
                 for g in range(passes):
                     c, g_in_chunk = divmod(g, CHUNK_PASSES)
-                    g0 = g - g % PASSES_PER_LOAD
                     offset = 4 * (g % PLANES_PER_TILE)
-                    nc.tensor.matmul_mx(
-                        out=acc[:],
-                        lhsT=x_codes[(c, m)][:, g_in_chunk, :].bitcast(FP8X4),
-                        lhsT_scale=x_scales[(c, m)][:, g_in_chunk, :],
-                        rhs=w_codes[(j, g0)][:, g - g0, :].bitcast(FP8X4),
-                        rhs_scale=w_planes[wi][
-                            offset:P, g // PLANES_PER_TILE, nt * N_TILE : (nt + 1) * N_TILE
-                        ],
-                        start=(g == 0),
-                        stop=(g == passes - 1),
+                    for i in range(BANKS):
+                        first = nb * BLOCK + i * BANK
+                        nc.tensor.matmul_mx(
+                            out=accs[i][:],
+                            lhsT=x_codes[(c, m)][:, g_in_chunk, :].bitcast(FP8X4),
+                            lhsT_scale=x_scales[(c, m)][:, g_in_chunk, :],
+                            rhs=w_codes[(b, g)][:, i * BANK : (i + 1) * BANK].bitcast(FP8X4),
+                            rhs_scale=w_planes[wi][offset:P, g // PLANES_PER_TILE, first : first + BANK],
+                            start=(g == 0),
+                            stop=(g == passes - 1),
+                        )
+                result = results.tile([P, BLOCK], F32, name="result")
+                for i in range(BANKS):
+                    cols = slice(i * BANK, (i + 1) * BANK)
+                    nc.vector.tensor_tensor(
+                        out=result[:, cols], in0=accs[i][:], in1=bias_all[:, cols], op=mybir.AluOpType.add
                     )
-                result = results.tile([P, N_TILE], F32, name="result")
-                nc.vector.tensor_tensor(out=result[:], in0=acc[:], in1=bias_all[:], op=mybir.AluOpType.add)
-                nc.sync.dma_start(
-                    out=out[m * P : (m + 1) * P, j * N_TILE : (j + 1) * N_TILE], in_=result[:]
-                )
+                nc.sync.dma_start(out=out[m * P : (m + 1) * P, b * BLOCK : (b + 1) * BLOCK], in_=result[:])
 
-        for j in range(LEAD):
-            load_for_col_tile(j)
-        sort_x_chunk(0)
-        for j in range(len(col_tiles)):
-            if j < X_CHUNKS:
-                quantise_x_chunk(j)
-            bias_all = spread_bias(j)
-            if j + 1 < X_CHUNKS:
-                sort_x_chunk(j + 1)
-            multiply_col_tile(j, bias_all)
-            if j + LEAD < len(col_tiles):
-                load_for_col_tile(j + LEAD)
+        for b in range(LEAD):
+            load_for_block(b)
+        sort_x_for_block(0)
+        for b in range(len(blocks)):
+            quantise_x_for_block(b)
+            bias_all = spread_bias(b)
+            if b + 1 < len(blocks):
+                sort_x_for_block(b + 1)
+            multiply_block(b, bias_all)
+            if b + LEAD < len(blocks):
+                load_for_block(b + LEAD)

@@ -21,7 +21,7 @@ K_CHUNK = 1024
 CHUNK_PASSES = K_CHUNK // K_PASS
 PLANES_PER_TILE = 4
 LEAD = 3
-RESULT_BUFS = 10
+RESULT_BUFS = 12
 
 FLOPS = 2 * TOKENS * (1024 * 1024 + 2048 * 1024 + 4096 * 2048)
 
@@ -43,8 +43,7 @@ def tile_mlinear_kernel(
         stage = ctx.enter_context(tc.tile_pool(name="stage", bufs=4))
         x_pool = ctx.enter_context(tc.tile_pool(name="x_pool", bufs=2 * TOKEN_TILES))
         results = ctx.enter_context(tc.tile_pool(name="results", bufs=RESULT_BUFS))
-        psum_xt = ctx.enter_context(tc.psum_pool(name="psum_xt", bufs=4))
-        psum_acc = ctx.enter_context(tc.psum_pool(name="psum_acc", bufs=4))
+        psum = ctx.enter_context(tc.psum_pool(name="psum", bufs=8))
         ctx.enter_context(tc.manual_schedule())
 
         x_rows = {}
@@ -116,7 +115,7 @@ def tile_mlinear_kernel(
         def quantise_x_for_block(b):
             for c in new_chunks[b]:
                 for m in range(TOKEN_TILES):
-                    xt = psum_xt.tile([P, CHUNK_PASSES, 2, P], F32, name="xt")
+                    xt = psum.tile([P, CHUNK_PASSES, 2, P], F32, name="bank")
                     for g in range(CHUNK_PASSES):
                         for u in range(2):
                             nc.tensor.transpose(xt[:, g, u, :], x_sorted[(c, m)][:, g, u, :], ident[:])
@@ -146,7 +145,7 @@ def tile_mlinear_kernel(
             bias_all = keep.tile([P, BLOCK], F32, name="bias_all_%d" % b)
             for i in range(BANKS):
                 first = b * BLOCK + i * BANK
-                bias_ps = psum_acc.tile([P, BANK], F32, name="acc")
+                bias_ps = psum.tile([P, BANK], F32, name="bank")
                 nc.tensor.matmul(
                     bias_ps[:], lhsT=ones[:], rhs=bias_row[:, first : first + BANK], start=True, stop=True
                 )
@@ -156,29 +155,35 @@ def tile_mlinear_kernel(
         def multiply_block(b, bias_all):
             wi, nb = blocks[b]
             passes = block_passes[b]
-            for m in range(TOKEN_TILES):
-                accs = [psum_acc.tile([P, BANK], F32, name="acc") for i in range(BANKS)]
-                for g in range(passes):
+            block_results = [results.tile([P, BLOCK], F32, name="result") for m in range(TOKEN_TILES)]
+            for i in range(BANKS):
+                accs = [psum.tile([P, BANK], F32, name="bank") for m in range(TOKEN_TILES)]
+                if i == 0:
+                    order = [(g, m) for g in range(passes) for m in range(TOKEN_TILES)]
+                else:
+                    order = [(g, m) for m in range(TOKEN_TILES) for g in range(passes)]
+                first = nb * BLOCK + i * BANK
+                cols = slice(i * BANK, (i + 1) * BANK)
+                for g, m in order:
                     c, g_in_chunk = divmod(g, CHUNK_PASSES)
                     offset = 4 * (g % PLANES_PER_TILE)
-                    for i in range(BANKS):
-                        first = nb * BLOCK + i * BANK
-                        nc.tensor.matmul_mx(
-                            out=accs[i][:],
-                            lhsT=x_codes[(c, m)][:, g_in_chunk, :].bitcast(FP8X4),
-                            lhsT_scale=x_scales[(c, m)][:, g_in_chunk, :],
-                            rhs=w_codes[(b, g)][:, i * BANK : (i + 1) * BANK].bitcast(FP8X4),
-                            rhs_scale=w_planes[wi][offset:P, g // PLANES_PER_TILE, first : first + BANK],
-                            start=(g == 0),
-                            stop=(g == passes - 1),
-                        )
-                result = results.tile([P, BLOCK], F32, name="result")
-                for i in range(BANKS):
-                    cols = slice(i * BANK, (i + 1) * BANK)
-                    nc.vector.tensor_tensor(
-                        out=result[:, cols], in0=accs[i][:], in1=bias_all[:, cols], op=mybir.AluOpType.add
+                    nc.tensor.matmul_mx(
+                        out=accs[m][:],
+                        lhsT=x_codes[(c, m)][:, g_in_chunk, :].bitcast(FP8X4),
+                        lhsT_scale=x_scales[(c, m)][:, g_in_chunk, :],
+                        rhs=w_codes[(b, g)][:, cols].bitcast(FP8X4),
+                        rhs_scale=w_planes[wi][offset:P, g // PLANES_PER_TILE, first : first + BANK],
+                        start=(g == 0),
+                        stop=(g == passes - 1),
                     )
-                nc.sync.dma_start(out=out[m * P : (m + 1) * P, b * BLOCK : (b + 1) * BLOCK], in_=result[:])
+                for m in range(TOKEN_TILES):
+                    nc.vector.tensor_tensor(
+                        out=block_results[m][:, cols], in0=accs[m][:], in1=bias_all[:, cols], op=mybir.AluOpType.add
+                    )
+                    if i == BANKS - 1:
+                        nc.sync.dma_start(
+                            out=out[m * P : (m + 1) * P, b * BLOCK : (b + 1) * BLOCK], in_=block_results[m][:]
+                        )
 
         for b in range(LEAD):
             load_for_block(b)

@@ -62,12 +62,14 @@ def tile_mlinear_kernel(
                 align_bytes=64,
             )
             w_planes.append(planes)
+        ones = keep.tile([P, P], BF16, name="ones")
+        nc.vector.memset(ones[:], 1.0)
+        table_warmer = keep.tile([P, 1], BF16, name="table_warmer")
+        nc.scalar.copy(out=table_warmer[:], in_=ones[:, 0:1])
         nc.vector.memset(w_planes[0][:].bitcast(I32), 0)
         bias_row = keep.tile([P, out.shape[1]], BF16, name="bias_row")
         nc.vector.memset(bias_row[:].bitcast(I32), 0)
         nc.scalar.dma_start(out=bias_row[0:1, :], in_=bias.rearrange("(o n) -> o n", o=1))
-        ones = keep.tile([P, P], BF16, name="ones")
-        nc.vector.memset(ones[:], 1.0)
         nc.vector.memset(w_planes[1][:].bitcast(I32), 0)
         nc.vector.memset(w_planes[2][:].bitcast(I32), 0)
         ident = keep.tile([P, P], F32, name="ident")
@@ -118,7 +120,13 @@ def tile_mlinear_kernel(
                     xt = psum.tile([P, CHUNK_PASSES, 2, P], F32, name="bank")
                     for g in range(CHUNK_PASSES):
                         for u in range(2):
-                            nc.tensor.transpose(xt[:, g, u, :], x_sorted[(c, m)][:, g, u, :], ident[:])
+                            if c == 0:
+                                words = x_rows[(c, m)][:].bitcast(F32)
+                                nc.tensor.transpose(
+                                    xt[:, g, u, :], words[:, 2 * P * g + u : 2 * P * (g + 1) : 2], ident[:]
+                                )
+                            else:
+                                nc.tensor.transpose(xt[:, g, u, :], x_sorted[(c, m)][:, g, u, :], ident[:])
                     grouped = stage.tile([P, CHUNK_PASSES * P * 4], BF16, name="grouped", align_bytes=64)
                     grouped_words = grouped[:].bitcast(F32).rearrange(
                         "p (g r u) -> p g r u", g=CHUNK_PASSES, u=2
@@ -187,7 +195,6 @@ def tile_mlinear_kernel(
 
         for b in range(LEAD):
             load_for_block(b)
-        sort_x_for_block(0)
         for b in range(len(blocks)):
             quantise_x_for_block(b)
             bias_all = spread_bias(b)

@@ -150,14 +150,18 @@ def tile_mlinear_kernel(
                     x_scales[(c, m)] = plane
 
         def spread_bias(b):
-            bias_all = keep.tile([P, BLOCK], F32, name="bias_all_%d" % b)
+            bias_ps = psum.tile([P, BLOCK], BF16, name="bank")
             for i in range(BANKS):
                 first = b * BLOCK + i * BANK
-                bias_ps = psum.tile([P, BANK], F32, name="bank")
                 nc.tensor.matmul(
-                    bias_ps[:], lhsT=ones[:], rhs=bias_row[:, first : first + BANK], start=True, stop=True
+                    bias_ps[:, i * BANK : (i + 1) * BANK],
+                    lhsT=ones[:],
+                    rhs=bias_row[:, first : first + BANK],
+                    start=True,
+                    stop=True,
                 )
-                nc.scalar.copy(out=bias_all[:, i * BANK : (i + 1) * BANK], in_=bias_ps[:])
+            bias_all = keep.tile([P, BLOCK], BF16, name="bias_all_%d" % b)
+            nc.scalar.copy(out=bias_all[:], in_=bias_ps[:])
             return bias_all
 
         def multiply_block(b, bias_all):
@@ -197,9 +201,10 @@ def tile_mlinear_kernel(
             load_for_block(b)
         for b in range(len(blocks)):
             quantise_x_for_block(b)
-            bias_all = spread_bias(b)
+            if b == 0:
+                bias_tiles = [spread_bias(j) for j in range(len(blocks))]
             if b + 1 < len(blocks):
                 sort_x_for_block(b + 1)
-            multiply_block(b, bias_all)
+            multiply_block(b, bias_tiles[b])
             if b + LEAD < len(blocks):
                 load_for_block(b + LEAD)

@@ -21,6 +21,7 @@ K_CHUNK = 1024
 CHUNK_PASSES = K_CHUNK // K_PASS
 PLANES_PER_TILE = 4
 LEAD = 3
+WARM_UP_MATMULS = 5
 RESULT_BUFS = 12
 
 FLOPS = 2 * TOKENS * (1024 * 1024 + 2048 * 1024 + 4096 * 2048)
@@ -62,8 +63,11 @@ def tile_mlinear_kernel(
                 align_bytes=64,
             )
             w_planes.append(planes)
-        ones = keep.tile([P, P], BF16, name="ones")
+        ones = keep.tile([P, BANK], BF16, name="ones")
         nc.vector.memset(ones[:], 1.0)
+        idle_ps = psum.tile([P, BANK], F32, name="bank")
+        for k in range(WARM_UP_MATMULS):
+            nc.tensor.matmul(idle_ps[:], lhsT=ones[:, 0:P], rhs=ones[:], start=True, stop=True)
         table_warmer = keep.tile([P, 1], BF16, name="table_warmer")
         nc.scalar.copy(out=table_warmer[:], in_=ones[:, 0:1])
         nc.vector.memset(w_planes[0][:].bitcast(I32), 0)
@@ -114,7 +118,19 @@ def tile_mlinear_kernel(
                     )
                     x_sorted[(c, m)] = sorted_words
 
-        def quantise_x_for_block(b):
+        def quantise_unit(c, m, grouped):
+            codes = keep.tile([P, CHUNK_PASSES, P], U32, name="x_codes_%d_%d" % (c, m), align_bytes=64)
+            plane = keep.tile([P, CHUNK_PASSES, P], U8, name="x_scales_%d_%d" % (c, m), align_bytes=64)
+            nc.vector.quantize_mx(
+                out=codes[:].rearrange("p g r -> p (g r)").bitcast(FP8X4),
+                scales=plane[:].rearrange("p g r -> p (g r)"),
+                in_=grouped[:],
+            )
+            x_codes[(c, m)] = codes
+            x_scales[(c, m)] = plane
+
+        def quantise_x_for_block(b, after_unit):
+            waiting = []
             for c in new_chunks[b]:
                 for m in range(TOKEN_TILES):
                     xt = psum.tile([P, CHUNK_PASSES, 2, P], F32, name="bank")
@@ -135,19 +151,12 @@ def tile_mlinear_kernel(
                         nc.scalar.copy(out=grouped_words, in_=xt[:].rearrange("p g u r -> p g r u"))
                     else:
                         nc.vector.tensor_copy(out=grouped_words, in_=xt[:].rearrange("p g u r -> p g r u"))
-                    codes = keep.tile(
-                        [P, CHUNK_PASSES, P], U32, name="x_codes_%d_%d" % (c, m), align_bytes=64
-                    )
-                    plane = keep.tile(
-                        [P, CHUNK_PASSES, P], U8, name="x_scales_%d_%d" % (c, m), align_bytes=64
-                    )
-                    nc.vector.quantize_mx(
-                        out=codes[:].rearrange("p g r -> p (g r)").bitcast(FP8X4),
-                        scales=plane[:].rearrange("p g r -> p (g r)"),
-                        in_=grouped[:],
-                    )
-                    x_codes[(c, m)] = codes
-                    x_scales[(c, m)] = plane
+                    for unit in waiting:
+                        quantise_unit(*unit)
+                    waiting = [(c, m, grouped)]
+                    after_unit(m)
+            for unit in waiting:
+                quantise_unit(*unit)
 
         def spread_bias(b):
             bias_ps = psum.tile([P, BLOCK], BF16, name="bank")
@@ -155,14 +164,14 @@ def tile_mlinear_kernel(
                 first = b * BLOCK + i * BANK
                 nc.tensor.matmul(
                     bias_ps[:, i * BANK : (i + 1) * BANK],
-                    lhsT=ones[:],
+                    lhsT=ones[:, 0:P],
                     rhs=bias_row[:, first : first + BANK],
                     start=True,
                     stop=True,
                 )
             bias_all = keep.tile([P, BLOCK], BF16, name="bias_all_%d" % b)
             nc.scalar.copy(out=bias_all[:], in_=bias_ps[:])
-            return bias_all
+            bias_tiles.append(bias_all)
 
         def multiply_block(b, bias_all):
             wi, nb = blocks[b]
@@ -199,10 +208,9 @@ def tile_mlinear_kernel(
 
         for b in range(LEAD):
             load_for_block(b)
+        bias_tiles = []
         for b in range(len(blocks)):
-            quantise_x_for_block(b)
-            if b == 0:
-                bias_tiles = [spread_bias(j) for j in range(len(blocks))]
+            quantise_x_for_block(b, spread_bias if b == 0 else (lambda m: None))
             if b + 1 < len(blocks):
                 sort_x_for_block(b + 1)
             multiply_block(b, bias_tiles[b])

@@ -63,6 +63,11 @@ def tile_mlinear_kernel(
                 align_bytes=64,
             )
             w_planes.append(planes)
+        bias_rows = keep.tile([P, BANK], BF16, name="bias_rows")
+        nc.vector.memset(bias_rows[:].bitcast(I32), 0)
+        nc.scalar.dma_start(
+            out=bias_rows[0 : out.shape[1] // BANK, :], in_=bias.rearrange("(j n) -> j n", n=BANK)
+        )
         ones = keep.tile([P, BANK], BF16, name="ones")
         nc.vector.memset(ones[:], 1.0)
         idle_ps = psum.tile([P, BANK], F32, name="bank")
@@ -71,13 +76,12 @@ def tile_mlinear_kernel(
         table_warmer = keep.tile([P, 1], BF16, name="table_warmer")
         nc.scalar.copy(out=table_warmer[:], in_=ones[:, 0:1])
         nc.vector.memset(w_planes[0][:].bitcast(I32), 0)
-        bias_row = keep.tile([P, out.shape[1]], BF16, name="bias_row")
-        nc.vector.memset(bias_row[:].bitcast(I32), 0)
-        nc.scalar.dma_start(out=bias_row[0:1, :], in_=bias.rearrange("(o n) -> o n", o=1))
         nc.vector.memset(w_planes[1][:].bitcast(I32), 0)
         nc.vector.memset(w_planes[2][:].bitcast(I32), 0)
         ident = keep.tile([P, P], F32, name="ident")
         make_identity(nc, ident[:])
+        ident_bf16 = keep.tile([P, P], BF16, name="ident_bf16")
+        nc.vector.tensor_copy(out=ident_bf16[:], in_=ident[:])
 
         def load_for_block(b):
             for c in new_chunks[b]:
@@ -161,11 +165,11 @@ def tile_mlinear_kernel(
         def spread_bias(b):
             bias_ps = psum.tile([P, BLOCK], BF16, name="bank")
             for i in range(BANKS):
-                first = b * BLOCK + i * BANK
+                j = b * BANKS + i
                 nc.tensor.matmul(
                     bias_ps[:, i * BANK : (i + 1) * BANK],
-                    lhsT=ones[:, 0:P],
-                    rhs=bias_row[:, first : first + BANK],
+                    lhsT=ident_bf16[:, j : j + 1].to_broadcast([P, P]),
+                    rhs=bias_rows[:],
                     start=True,
                     stop=True,
                 )

@@ -22,6 +22,8 @@ CHUNK_PASSES = K_CHUNK // K_PASS
 PLANES_PER_TILE = 4
 LEAD = 3
 WARM_UP_MATMULS = 5
+BIAS_BEHIND_TOKEN_TILE = {1: [1], 3: [2, 3]}
+MX_ALIGN = 256
 RESULT_BUFS = 12
 
 FLOPS = 2 * TOKENS * (1024 * 1024 + 2048 * 1024 + 4096 * 2048)
@@ -60,7 +62,7 @@ def tile_mlinear_kernel(
                 [P, (passes + PLANES_PER_TILE - 1) // PLANES_PER_TILE, columns],
                 U8,
                 name="w%d_planes" % wi,
-                align_bytes=64,
+                align_bytes=MX_ALIGN,
             )
             w_planes.append(planes)
         bias_rows = keep.tile([P, BANK], BF16, name="bias_rows")
@@ -69,7 +71,7 @@ def tile_mlinear_kernel(
             out=bias_rows[0 : out.shape[1] // BANK, :], in_=bias.rearrange("(j n) -> j n", n=BANK)
         )
         ones = keep.tile([P, BANK], BF16, name="ones")
-        nc.vector.memset(ones[:], 1.0)
+        nc.gpsimd.memset(ones[:], 1.0)
         idle_ps = psum.tile([P, BANK], F32, name="bank")
         for k in range(WARM_UP_MATMULS):
             nc.tensor.matmul(idle_ps[:], lhsT=ones[:, 0:P], rhs=ones[:], start=True, stop=True)
@@ -105,7 +107,7 @@ def tile_mlinear_kernel(
                             in_=scale_words[h : h + count, 4 * quadrant : 4 * quadrant + 4, :],
                         )
             for g in range(passes):
-                codes = keep.tile([P, BLOCK], U32, name="w_codes_%d_%d" % (b, g), align_bytes=64)
+                codes = keep.tile([P, BLOCK], U32, name="w_codes_%d_%d" % (b, g), align_bytes=MX_ALIGN)
                 nc.sync.dma_start(
                     out=codes[:].bitcast(I32),
                     in_=words[g].rearrange("p n t -> p (n t)").bitcast(I32)[:, nb * BLOCK : (nb + 1) * BLOCK],
@@ -123,8 +125,8 @@ def tile_mlinear_kernel(
                     x_sorted[(c, m)] = sorted_words
 
         def quantise_unit(c, m, grouped):
-            codes = keep.tile([P, CHUNK_PASSES, P], U32, name="x_codes_%d_%d" % (c, m), align_bytes=64)
-            plane = keep.tile([P, CHUNK_PASSES, P], U8, name="x_scales_%d_%d" % (c, m), align_bytes=64)
+            codes = keep.tile([P, CHUNK_PASSES, P], U32, name="x_codes_%d_%d" % (c, m), align_bytes=MX_ALIGN)
+            plane = keep.tile([P, CHUNK_PASSES, P], U8, name="x_scales_%d_%d" % (c, m), align_bytes=MX_ALIGN)
             nc.vector.quantize_mx(
                 out=codes[:].rearrange("p g r -> p (g r)").bitcast(FP8X4),
                 scales=plane[:].rearrange("p g r -> p (g r)"),
@@ -174,8 +176,15 @@ def tile_mlinear_kernel(
                     stop=True,
                 )
             bias_all = keep.tile([P, BLOCK], BF16, name="bias_all_%d" % b)
-            nc.scalar.copy(out=bias_all[:], in_=bias_ps[:])
+            if b == 0:
+                nc.vector.tensor_copy(out=bias_all[:], in_=bias_ps[:])
+            else:
+                nc.scalar.copy(out=bias_all[:], in_=bias_ps[:])
             bias_tiles.append(bias_all)
+
+        def spread_bias_in_head(m):
+            for b in BIAS_BEHIND_TOKEN_TILE.get(m, []):
+                spread_bias(b)
 
         def multiply_block(b, bias_all):
             wi, nb = blocks[b]
@@ -214,7 +223,9 @@ def tile_mlinear_kernel(
             load_for_block(b)
         bias_tiles = []
         for b in range(len(blocks)):
-            quantise_x_for_block(b, spread_bias if b == 0 else (lambda m: None))
+            if b == 0:
+                spread_bias(0)
+            quantise_x_for_block(b, spread_bias_in_head if b == 0 else (lambda m: None))
             if b + 1 < len(blocks):
                 sort_x_for_block(b + 1)
             multiply_block(b, bias_tiles[b])

@@ -190,34 +190,65 @@ def tile_mlinear_kernel(
             wi, nb = blocks[b]
             passes = block_passes[b]
             block_results = [results.tile([P, BLOCK], F32, name="result") for m in range(TOKEN_TILES)]
+
+            def one_pass(b, g, m, cols, acc):
+                c, g_in_chunk = divmod(g, CHUNK_PASSES)
+                offset = 4 * (g % PLANES_PER_TILE)
+                nc.tensor.matmul_mx(
+                    out=acc,
+                    lhsT=x_codes[(c, m)][:, g_in_chunk, :].bitcast(FP8X4),
+                    lhsT_scale=x_scales[(c, m)][:, g_in_chunk, :],
+                    rhs=w_codes[(b, g)][:, cols].bitcast(FP8X4),
+                    rhs_scale=w_planes[wi][
+                        offset:P, g // PLANES_PER_TILE, nb * BLOCK + cols.start : nb * BLOCK + cols.stop
+                    ],
+                    start=(g == 0),
+                    stop=(g == passes - 1),
+                )
+
+            def finish(b, m, cols, acc):
+                nc.vector.tensor_tensor(
+                    out=block_results[m][:, cols], in0=acc, in1=bias_all[:, cols], op=mybir.AluOpType.add
+                )
+
+            def store(b, m, cols):
+                nc.sync.dma_start(
+                    out=out[m * P : (m + 1) * P, b * BLOCK + cols.start : b * BLOCK + cols.stop],
+                    in_=block_results[m][:, cols],
+                )
+
             for i in range(BANKS):
                 accs = [psum.tile([P, BANK], F32, name="bank") for m in range(TOKEN_TILES)]
                 if i == 0:
                     order = [(g, m) for g in range(passes) for m in range(TOKEN_TILES)]
                 else:
                     order = [(g, m) for m in range(TOKEN_TILES) for g in range(passes)]
-                first = nb * BLOCK + i * BANK
                 cols = slice(i * BANK, (i + 1) * BANK)
+                end_pieces = []
+                if b == len(blocks) - 1 and i == BANKS - 1:
+                    order = order[:-passes]
                 for g, m in order:
-                    c, g_in_chunk = divmod(g, CHUNK_PASSES)
-                    offset = 4 * (g % PLANES_PER_TILE)
-                    nc.tensor.matmul_mx(
-                        out=accs[m][:],
-                        lhsT=x_codes[(c, m)][:, g_in_chunk, :].bitcast(FP8X4),
-                        lhsT_scale=x_scales[(c, m)][:, g_in_chunk, :],
-                        rhs=w_codes[(b, g)][:, cols].bitcast(FP8X4),
-                        rhs_scale=w_planes[wi][offset:P, g // PLANES_PER_TILE, first : first + BANK],
-                        start=(g == 0),
-                        stop=(g == passes - 1),
-                    )
+                    one_pass(b, g, m, cols, accs[m][:])
+                if b == len(blocks) - 1 and i == BANKS - 1:
+                    m = TOKEN_TILES - 1
+                    for half in range(2):
+                        acc = accs[m] if half == 0 else psum.tile([P, BANK], F32, name="bank")
+                        piece = slice(i * BANK + half * (BANK // 2), i * BANK + (half + 1) * (BANK // 2))
+                        for g in range(passes):
+                            one_pass(b, g, m, piece, acc[:, 0 : BANK // 2])
+                        end_pieces.append((piece, acc))
                 for m in range(TOKEN_TILES):
-                    nc.vector.tensor_tensor(
-                        out=block_results[m][:, cols], in0=accs[m][:], in1=bias_all[:, cols], op=mybir.AluOpType.add
-                    )
-                    if i == BANKS - 1:
-                        nc.sync.dma_start(
-                            out=out[m * P : (m + 1) * P, b * BLOCK : (b + 1) * BLOCK], in_=block_results[m][:]
-                        )
+                    is_end = b == len(blocks) - 1 and m == TOKEN_TILES - 1
+                    if is_end and i == BANKS - 1:
+                        for piece, acc in end_pieces:
+                            finish(b, m, piece, acc[:, 0 : BANK // 2])
+                            store(b, m, piece)
+                        continue
+                    finish(b, m, cols, accs[m][:])
+                    if is_end:
+                        store(b, m, cols)
+                    elif i == BANKS - 1:
+                        store(b, m, slice(0, BLOCK))
 
         for b in range(LEAD):
             load_for_block(b)

@@ -22,7 +22,9 @@ CHUNK_PASSES = K_CHUNK // K_PASS
 PLANES_PER_TILE = 4
 LEAD = 3
 WARM_UP_MATMULS = 5
-BIAS_BEHIND_TOKEN_TILE = {1: [1], 3: [2, 3]}
+WARM_BEHIND_TOKEN_TILE = {1: 2, 3: 2}
+SQUARE = 32
+BLOCKS_BY_GROUPS = (0, 2)
 MX_ALIGN = 256
 RESULT_BUFS = 12
 
@@ -65,10 +67,11 @@ def tile_mlinear_kernel(
                 align_bytes=MX_ALIGN,
             )
             w_planes.append(planes)
-        bias_rows = keep.tile([P, BANK], BF16, name="bias_rows")
+        bias_rows = keep.tile([P, SQUARE], F32, name="bias_rows")
         nc.vector.memset(bias_rows[:].bitcast(I32), 0)
         nc.scalar.dma_start(
-            out=bias_rows[0 : out.shape[1] // BANK, :], in_=bias.rearrange("(j n) -> j n", n=BANK)
+            out=bias_rows[0 : out.shape[1] // (2 * SQUARE), :].bitcast(BF16),
+            in_=bias.rearrange("(j n) -> j n", n=2 * SQUARE),
         )
         ones = keep.tile([P, BANK], BF16, name="ones")
         nc.gpsimd.memset(ones[:], 1.0)
@@ -82,8 +85,6 @@ def tile_mlinear_kernel(
         nc.vector.memset(w_planes[2][:].bitcast(I32), 0)
         ident = keep.tile([P, P], F32, name="ident")
         make_identity(nc, ident[:])
-        ident_bf16 = keep.tile([P, P], BF16, name="ident_bf16")
-        nc.vector.tensor_copy(out=ident_bf16[:], in_=ident[:])
 
         def load_for_block(b):
             for c in new_chunks[b]:
@@ -106,13 +107,16 @@ def tile_mlinear_kernel(
                             out=w_planes[wi][first : first + 4 * count, h // PLANES_PER_TILE, :].bitcast(I32),
                             in_=scale_words[h : h + count, 4 * quadrant : 4 * quadrant + 4, :],
                         )
+            width = BANK if b in BLOCKS_BY_GROUPS else BLOCK
             for g in range(passes):
-                codes = keep.tile([P, BLOCK], U32, name="w_codes_%d_%d" % (b, g), align_bytes=MX_ALIGN)
-                nc.sync.dma_start(
-                    out=codes[:].bitcast(I32),
-                    in_=words[g].rearrange("p n t -> p (n t)").bitcast(I32)[:, nb * BLOCK : (nb + 1) * BLOCK],
-                )
-                w_codes[(b, g)] = codes
+                w_codes[(b, g)] = keep.tile([P, BLOCK], U32, name="w_codes_%d_%d" % (b, g), align_bytes=MX_ALIGN)
+            for first in range(0, BLOCK, width):
+                for g in range(passes):
+                    word_rows = words[g].rearrange("p n t -> p (n t)").bitcast(I32)
+                    nc.sync.dma_start(
+                        out=w_codes[(b, g)][:, first : first + width].bitcast(I32),
+                        in_=word_rows[:, nb * BLOCK + first : nb * BLOCK + first + width],
+                    )
 
         def sort_x_for_block(b):
             for c in new_chunks[b]:
@@ -164,27 +168,33 @@ def tile_mlinear_kernel(
             for unit in waiting:
                 quantise_unit(*unit)
 
-        def spread_bias(b):
-            bias_ps = psum.tile([P, BLOCK], BF16, name="bank")
-            for i in range(BANKS):
-                j = b * BANKS + i
-                nc.tensor.matmul(
-                    bias_ps[:, i * BANK : (i + 1) * BANK],
-                    lhsT=ident_bf16[:, j : j + 1].to_broadcast([P, P]),
-                    rhs=bias_rows[:],
-                    start=True,
-                    stop=True,
-                )
-            bias_all = keep.tile([P, BLOCK], BF16, name="bias_all_%d" % b)
-            if b == 0:
-                nc.vector.tensor_copy(out=bias_all[:], in_=bias_ps[:])
-            else:
-                nc.scalar.copy(out=bias_all[:], in_=bias_ps[:])
-            bias_tiles.append(bias_all)
+        bias_columns = keep.tile([P, P], F32, name="bias_columns")
 
-        def spread_bias_in_head(m):
-            for b in BIAS_BEHIND_TOKEN_TILE.get(m, []):
-                spread_bias(b)
+        def turn_bias():
+            bias_rows_x4 = keep.tile([P, P // SQUARE, SQUARE], F32, name="bias_rows_x4")
+            nc.gpsimd.tensor_copy(
+                out=bias_rows_x4[:], in_=bias_rows[:].unsqueeze(1).to_broadcast([P, P // SQUARE, SQUARE])
+            )
+            bias_ps = psum.tile([P, P], F32, name="bank")
+            nc.tensor.transpose(bias_ps[:], bias_rows_x4[:].rearrange("p q w -> p (q w)"), ident[:])
+            nc.scalar.copy(out=bias_columns[:], in_=bias_ps[:])
+
+        def spread_bias(b):
+            rows = BLOCK // (2 * SQUARE)
+            repeated = stage.tile([P, rows, SQUARE], F32, name="repeated", align_bytes=64)
+            nc.scalar.copy(
+                out=repeated[:],
+                in_=bias_columns[:, b * rows : (b + 1) * rows].unsqueeze(2).to_broadcast([P, rows, SQUARE]),
+            )
+            bias_words = keep.tile([P, rows * SQUARE], F32, name="bias_words_%d" % b, align_bytes=64)
+            nc.vector.transpose(out=bias_words[:], in_=repeated[:].rearrange("p j w -> p (j w)"))
+            return bias_words[:].bitcast(BF16)
+
+        def fill_head(m):
+            if m == TOKEN_TILES - 1:
+                turn_bias()
+            for k in range(WARM_BEHIND_TOKEN_TILE.get(m, 0)):
+                nc.tensor.matmul(idle_ps[:], lhsT=ones[:, 0:P], rhs=ones[:], start=True, stop=True)
 
         def multiply_block(b, bias_all):
             wi, nb = blocks[b]
@@ -252,13 +262,11 @@ def tile_mlinear_kernel(
 
         for b in range(LEAD):
             load_for_block(b)
-        bias_tiles = []
         for b in range(len(blocks)):
-            if b == 0:
-                spread_bias(0)
-            quantise_x_for_block(b, spread_bias_in_head if b == 0 else (lambda m: None))
+            quantise_x_for_block(b, fill_head if b == 0 else (lambda m: None))
+            bias_all = spread_bias(b)
             if b + 1 < len(blocks):
                 sort_x_for_block(b + 1)
-            multiply_block(b, bias_tiles[b])
+            multiply_block(b, bias_all)
             if b + LEAD < len(blocks):
                 load_for_block(b + LEAD)

@@ -22,7 +22,7 @@ CHUNK_PASSES = K_CHUNK // K_PASS
 PLANES_PER_TILE = 4
 LEAD = 3
 WARM_UP_MATMULS = 5
-WARM_BEHIND_TOKEN_TILE = {1: 2, 3: 2}
+WARM_BEHIND_TOKEN_TILE = {1: 3, 3: 3}
 SQUARE = 32
 BLOCKS_BY_GROUPS = (0, 2)
 MX_ALIGN = 256
@@ -118,15 +118,16 @@ def tile_mlinear_kernel(
                         in_=word_rows[:, nb * BLOCK + first : nb * BLOCK + first + width],
                     )
 
+        def sort_x(c, m, copy):
+            pairs = x_rows[(c, m)][:].bitcast(F32)
+            sorted_words = x_pool.tile([P, CHUNK_PASSES, 2, P], F32, name="sorted_words")
+            copy(out=sorted_words[:], in_=pairs.rearrange("r (g p u) -> r g u p", g=CHUNK_PASSES, u=2))
+            x_sorted[(c, m)] = sorted_words
+
         def sort_x_for_block(b):
             for c in new_chunks[b]:
                 for m in range(TOKEN_TILES):
-                    pairs = x_rows[(c, m)][:].bitcast(F32)
-                    sorted_words = x_pool.tile([P, CHUNK_PASSES, 2, P], F32, name="sorted_words")
-                    nc.scalar.copy(
-                        out=sorted_words[:], in_=pairs.rearrange("r (g p u) -> r g u p", g=CHUNK_PASSES, u=2)
-                    )
-                    x_sorted[(c, m)] = sorted_words
+                    sort_x(c, m, nc.scalar.copy)
 
         def quantise_unit(c, m, grouped):
             codes = keep.tile([P, CHUNK_PASSES, P], U32, name="x_codes_%d_%d" % (c, m), align_bytes=MX_ALIGN)
@@ -146,7 +147,7 @@ def tile_mlinear_kernel(
                     xt = psum.tile([P, CHUNK_PASSES, 2, P], F32, name="bank")
                     for g in range(CHUNK_PASSES):
                         for u in range(2):
-                            if c == 0:
+                            if (c, m) not in x_sorted:
                                 words = x_rows[(c, m)][:].bitcast(F32)
                                 nc.tensor.transpose(
                                     xt[:, g, u, :], words[:, 2 * P * g + u : 2 * P * (g + 1) : 2], ident[:]
@@ -161,6 +162,10 @@ def tile_mlinear_kernel(
                         nc.scalar.copy(out=grouped_words, in_=xt[:].rearrange("p g u r -> p g r u"))
                     else:
                         nc.vector.tensor_copy(out=grouped_words, in_=xt[:].rearrange("p g u r -> p g r u"))
+                    if c == 0 and m == 0:
+                        sort_x(0, 2, nc.scalar.copy)
+                    if c == 0 and m == 1:
+                        sort_x(0, 3, nc.vector.tensor_copy)
                     for unit in waiting:
                         quantise_unit(*unit)
                     waiting = [(c, m, grouped)]

from contextlib import ExitStack

import concourse.mybir as mybir
from concourse.masks import make_identity

F32 = mybir.dt.float32
BF16 = mybir.dt.bfloat16
I32 = mybir.dt.int32
U32 = mybir.dt.uint32
U8 = mybir.dt.uint8
FP8X4 = mybir.dt.float8_e4m3fn_x4

P = 128
K_PASS = 512
BANK = 512
BLOCK = 1024
BANKS = BLOCK // BANK
TOKENS = 512
TOKEN_TILES = TOKENS // P
K_CHUNK = 1024
CHUNK_PASSES = K_CHUNK // K_PASS
PLANES_PER_TILE = 4
LEAD = 3
WARM_UP_MATMULS = 5
WARM_BEHIND_TOKEN_TILE = {1: 3, 3: 3}
SQUARE = 32
BLOCKS_BY_GROUPS = (0, 2)
MX_ALIGN = 256
RESULT_BUFS = 12

FLOPS = 2 * TOKENS * (1024 * 1024 + 2048 * 1024 + 4096 * 2048)


def tile_mlinear_kernel(
    tc, x, w0_words, w0_scales, w1_words, w1_scales, w2_words, w2_scales, bias, out
):
    nc = tc.nc
    weights = [(w0_words, w0_scales), (w1_words, w1_scales), (w2_words, w2_scales)]
    blocks = [(wi, nb) for wi in range(len(weights)) for nb in range(weights[wi][0].shape[2] // BLOCK)]
    block_passes = [weights[wi][0].shape[0] for wi, nb in blocks]
    new_chunks = [
        range(0 if b == 0 else block_passes[b - 1] // CHUNK_PASSES, block_passes[b] // CHUNK_PASSES)
        for b in range(len(blocks))
    ]

    with ExitStack() as ctx:
        keep = ctx.enter_context(tc.tile_pool(name="keep", bufs=1))
        stage = ctx.enter_context(tc.tile_pool(name="stage", bufs=4))
        x_pool = ctx.enter_context(tc.tile_pool(name="x_pool", bufs=2 * TOKEN_TILES))
        results = ctx.enter_context(tc.tile_pool(name="results", bufs=RESULT_BUFS))
        psum = ctx.enter_context(tc.psum_pool(name="psum", bufs=8))
        ctx.enter_context(tc.manual_schedule())

        x_rows = {}
        x_sorted = {}
        x_codes = {}
        x_scales = {}
        w_codes = {}
        w_planes = []

        for wi in range(len(weights)):
            passes, columns = weights[wi][0].shape[0], weights[wi][0].shape[2]
            planes = keep.tile(
                [P, (passes + PLANES_PER_TILE - 1) // PLANES_PER_TILE, columns],
                U8,
                name="w%d_planes" % wi,
                align_bytes=MX_ALIGN,
            )
            w_planes.append(planes)
        bias_rows = keep.tile([P, SQUARE], F32, name="bias_rows")
        nc.vector.memset(bias_rows[:].bitcast(I32), 0)
        nc.scalar.dma_start(
            out=bias_rows[0 : out.shape[1] // (2 * SQUARE), :].bitcast(BF16),
            in_=bias.rearrange("(j n) -> j n", n=2 * SQUARE),
        )
        ones = keep.tile([P, BANK], BF16, name="ones")
        nc.gpsimd.memset(ones[:], 1.0)
        idle_ps = psum.tile([P, BANK], F32, name="bank")
        for k in range(WARM_UP_MATMULS):
            nc.tensor.matmul(idle_ps[:], lhsT=ones[:, 0:P], rhs=ones[:], start=True, stop=True)
        table_warmer = keep.tile([P, 1], BF16, name="table_warmer")
        nc.scalar.copy(out=table_warmer[:], in_=ones[:, 0:1])
        nc.vector.memset(w_planes[0][:].bitcast(I32), 0)
        nc.vector.memset(w_planes[1][:].bitcast(I32), 0)
        nc.vector.memset(w_planes[2][:].bitcast(I32), 0)
        ident = keep.tile([P, P], F32, name="ident")
        make_identity(nc, ident[:])

        def load_for_block(b):
            for c in new_chunks[b]:
                for m in range(TOKEN_TILES):
                    rows = x_pool.tile([P, K_CHUNK], BF16, name="rows")
                    nc.sync.dma_start(
                        out=rows[:], in_=x[m * P : (m + 1) * P, c * K_CHUNK : (c + 1) * K_CHUNK]
                    )
                    x_rows[(c, m)] = rows
            wi, nb = blocks[b]
            words, scales = weights[wi]
            passes = block_passes[b]
            if nb == 0:
                scale_words = scales.bitcast(I32)
                for h in range(0, passes, PLANES_PER_TILE):
                    count = min(PLANES_PER_TILE, passes - h)
                    for quadrant in range(4):
                        first = 32 * quadrant
                        nc.sync.dma_start(
                            out=w_planes[wi][first : first + 4 * count, h // PLANES_PER_TILE, :].bitcast(I32),
                            in_=scale_words[h : h + count, 4 * quadrant : 4 * quadrant + 4, :],
                        )
            width = BANK if b in BLOCKS_BY_GROUPS else BLOCK
            for g in range(passes):
                w_codes[(b, g)] = keep.tile([P, BLOCK], U32, name="w_codes_%d_%d" % (b, g), align_bytes=MX_ALIGN)
            for first in range(0, BLOCK, width):
                for g in range(passes):
                    word_rows = words[g].rearrange("p n t -> p (n t)").bitcast(I32)
                    nc.sync.dma_start(
                        out=w_codes[(b, g)][:, first : first + width].bitcast(I32),
                        in_=word_rows[:, nb * BLOCK + first : nb * BLOCK + first + width],
                    )

        def sort_x(c, m, copy):
            pairs = x_rows[(c, m)][:].bitcast(F32)
            sorted_words = x_pool.tile([P, CHUNK_PASSES, 2, P], F32, name="sorted_words")
            copy(out=sorted_words[:], in_=pairs.rearrange("r (g p u) -> r g u p", g=CHUNK_PASSES, u=2))
            x_sorted[(c, m)] = sorted_words

        def sort_x_for_block(b):
            for c in new_chunks[b]:
                for m in range(TOKEN_TILES):
                    sort_x(c, m, nc.scalar.copy)

        def quantise_unit(c, m, grouped):
            codes = keep.tile([P, CHUNK_PASSES, P], U32, name="x_codes_%d_%d" % (c, m), align_bytes=MX_ALIGN)
            plane = keep.tile([P, CHUNK_PASSES, P], U8, name="x_scales_%d_%d" % (c, m), align_bytes=MX_ALIGN)
            nc.vector.quantize_mx(
                out=codes[:].rearrange("p g r -> p (g r)").bitcast(FP8X4),
                scales=plane[:].rearrange("p g r -> p (g r)"),
                in_=grouped[:],
            )
            x_codes[(c, m)] = codes
            x_scales[(c, m)] = plane

        def quantise_x_for_block(b, after_unit):
            waiting = []
            for c in new_chunks[b]:
                for m in range(TOKEN_TILES):
                    xt = psum.tile([P, CHUNK_PASSES, 2, P], F32, name="bank")
                    for g in range(CHUNK_PASSES):
                        for u in range(2):
                            if (c, m) not in x_sorted:
                                words = x_rows[(c, m)][:].bitcast(F32)
                                nc.tensor.transpose(
                                    xt[:, g, u, :], words[:, 2 * P * g + u : 2 * P * (g + 1) : 2], ident[:]
                                )
                            else:
                                nc.tensor.transpose(xt[:, g, u, :], x_sorted[(c, m)][:, g, u, :], ident[:])
                    grouped = stage.tile([P, CHUNK_PASSES * P * 4], BF16, name="grouped", align_bytes=64)
                    grouped_words = grouped[:].bitcast(F32).rearrange(
                        "p (g r u) -> p g r u", g=CHUNK_PASSES, u=2
                    )
                    if m % 2 == 0:
                        nc.scalar.copy(out=grouped_words, in_=xt[:].rearrange("p g u r -> p g r u"))
                    else:
                        nc.vector.tensor_copy(out=grouped_words, in_=xt[:].rearrange("p g u r -> p g r u"))
                    if c == 0 and m == 0:
                        sort_x(0, 2, nc.scalar.copy)
                    if c == 0 and m == 1:
                        sort_x(0, 3, nc.vector.tensor_copy)
                    for unit in waiting:
                        quantise_unit(*unit)
                    waiting = [(c, m, grouped)]
                    after_unit(m)
            for unit in waiting:
                quantise_unit(*unit)

        bias_columns = keep.tile([P, P], F32, name="bias_columns")

        def turn_bias():
            bias_rows_x4 = keep.tile([P, P // SQUARE, SQUARE], F32, name="bias_rows_x4")
            nc.gpsimd.tensor_copy(
                out=bias_rows_x4[:], in_=bias_rows[:].unsqueeze(1).to_broadcast([P, P // SQUARE, SQUARE])
            )
            bias_ps = psum.tile([P, P], F32, name="bank")
            nc.tensor.transpose(bias_ps[:], bias_rows_x4[:].rearrange("p q w -> p (q w)"), ident[:])
            nc.scalar.copy(out=bias_columns[:], in_=bias_ps[:])

        def spread_bias(b):
            rows = BLOCK // (2 * SQUARE)
            repeated = stage.tile([P, rows, SQUARE], F32, name="repeated", align_bytes=64)
            nc.scalar.copy(
                out=repeated[:],
                in_=bias_columns[:, b * rows : (b + 1) * rows].unsqueeze(2).to_broadcast([P, rows, SQUARE]),
            )
            bias_words = keep.tile([P, rows * SQUARE], F32, name="bias_words_%d" % b, align_bytes=64)
            nc.vector.transpose(out=bias_words[:], in_=repeated[:].rearrange("p j w -> p (j w)"))
            return bias_words[:].bitcast(BF16)

        def fill_head(m):
            if m == TOKEN_TILES - 1:
                turn_bias()
            for k in range(WARM_BEHIND_TOKEN_TILE.get(m, 0)):
                nc.tensor.matmul(idle_ps[:], lhsT=ones[:, 0:P], rhs=ones[:], start=True, stop=True)

        def multiply_block(b, bias_all):
            wi, nb = blocks[b]
            passes = block_passes[b]
            block_results = [results.tile([P, BLOCK], F32, name="result") for m in range(TOKEN_TILES)]

            def one_pass(b, g, m, cols, acc):
                c, g_in_chunk = divmod(g, CHUNK_PASSES)
                offset = 4 * (g % PLANES_PER_TILE)
                nc.tensor.matmul_mx(
                    out=acc,
                    lhsT=x_codes[(c, m)][:, g_in_chunk, :].bitcast(FP8X4),
                    lhsT_scale=x_scales[(c, m)][:, g_in_chunk, :],
                    rhs=w_codes[(b, g)][:, cols].bitcast(FP8X4),
                    rhs_scale=w_planes[wi][
                        offset:P, g // PLANES_PER_TILE, nb * BLOCK + cols.start : nb * BLOCK + cols.stop
                    ],
                    start=(g == 0),
                    stop=(g == passes - 1),
                )

            def finish(b, m, cols, acc):
                nc.vector.tensor_tensor(
                    out=block_results[m][:, cols], in0=acc, in1=bias_all[:, cols], op=mybir.AluOpType.add
                )

            def store(b, m, cols):
                nc.sync.dma_start(
                    out=out[m * P : (m + 1) * P, b * BLOCK + cols.start : b * BLOCK + cols.stop],
                    in_=block_results[m][:, cols],
                )

            for i in range(BANKS):
                accs = [psum.tile([P, BANK], F32, name="bank") for m in range(TOKEN_TILES)]
                if i == 0:
                    order = [(g, m) for g in range(passes) for m in range(TOKEN_TILES)]
                else:
                    order = [(g, m) for m in range(TOKEN_TILES) for g in range(passes)]
                cols = slice(i * BANK, (i + 1) * BANK)
                end_pieces = []
                if b == len(blocks) - 1 and i == BANKS - 1:
                    order = order[:-passes]
                for g, m in order:
                    one_pass(b, g, m, cols, accs[m][:])
                if b == len(blocks) - 1 and i == BANKS - 1:
                    m = TOKEN_TILES - 1
                    for half in range(2):
                        acc = accs[m] if half == 0 else psum.tile([P, BANK], F32, name="bank")
                        piece = slice(i * BANK + half * (BANK // 2), i * BANK + (half + 1) * (BANK // 2))
                        for g in range(passes):
                            one_pass(b, g, m, piece, acc[:, 0 : BANK // 2])
                        end_pieces.append((piece, acc))
                for m in range(TOKEN_TILES):
                    is_end = b == len(blocks) - 1 and m == TOKEN_TILES - 1
                    if is_end and i == BANKS - 1:
                        for piece, acc in end_pieces:
                            finish(b, m, piece, acc[:, 0 : BANK // 2])
                            store(b, m, piece)
                        continue
                    finish(b, m, cols, accs[m][:])
                    if is_end:
                        store(b, m, cols)
                    elif i == BANKS - 1:
                        store(b, m, slice(0, BLOCK))

        for b in range(LEAD):
            load_for_block(b)
        for b in range(len(blocks)):
            quantise_x_for_block(b, fill_head if b == 0 else (lambda m: None))
            bias_all = spread_bias(b)
            if b + 1 < len(blocks):
                sort_x_for_block(b + 1)
            multiply_block(b, bias_all)
            if b + LEAD < len(blocks):
                load_for_block(b + LEAD)
